import numpy as np
import ml_dtypes


def mxq(x, axis, fmt="e4m3"):
    dtype, down = {"e4m3": (ml_dtypes.float8_e4m3fn, 7), "e5m2": (ml_dtypes.float8_e5m2, 14)}[fmt]
    v = np.moveaxis(np.asarray(x, np.float32).astype(ml_dtypes.bfloat16).astype(np.float64), axis, -1)
    blocks = v.reshape(v.shape[:-1] + (-1, 32))
    amax = np.abs(blocks).max(-1, keepdims=True)
    byte = np.maximum(np.where(amax > 0, np.frexp(amax)[1] - 1 + 127, 0) - down, 1)
    scale = np.exp2(byte - 127.0)
    codes = (blocks / scale).astype(np.float32).astype(dtype).astype(np.float64)
    return np.moveaxis((codes * scale).reshape(v.shape), -1, axis)


WIDE = False


def mx_kscale(k):
    if not WIDE:
        return np.ones(k)
    levels = np.array([10, -10, 5, -5, 0])
    a = np.random.permutation(np.resize(levels, k // 512 * 4)).reshape(k // 512, 4)
    idx = np.arange(k)
    return np.exp2(a[idx // 512, idx % 128 // 32])


BF16 = ml_dtypes.bfloat16


def bf(x):
    return np.asarray(x, np.float32).astype(BF16)


def f64(x):
    return np.asarray(x).astype(np.float64)


B, L, C, H, BLK = 8, 512, 512, 8, 128
D = C // H
MAX_SCALE_MUL = np.log(100.0)
EPS = 1e-12


def l2norm(t):
    n = np.sqrt(np.sum(t * t, axis=-1, keepdims=True))
    return t / np.maximum(n, EPS)


def setup_inputs():
    s = mx_kscale(C)
    lsm = np.linspace(np.log(4.0), MAX_SCALE_MUL + 1.0, H) + 0.05 * np.random.standard_normal(H)
    return {"x": bf(np.random.standard_normal((B, L, C)) * s),
            "W_qkv": bf(np.random.standard_normal((3 * C, C)) / np.sqrt(C) / s[None, :]),
            "q_bias": bf(np.random.standard_normal(C) * 0.3),
            "v_bias": bf(np.random.standard_normal(C) * 0.3),
            "log_scale_mul": bf(lsm.reshape(1, H, 1, 1))}


def reference(x, W_qkv, q_bias, v_bias, log_scale_mul):
    qb = f64(q_bias)
    bias = np.concatenate([qb, np.zeros_like(qb), f64(v_bias)])
    qkv = (mxq(f64(x), 2, "e4m3") @ mxq(f64(W_qkv), 1, "e4m3").T) + bias
    qkv = qkv.reshape(B, L, 3, H, D)
    q, k, v = np.moveaxis(qkv, 2, 0)
    q = np.swapaxes(q, 1, 2)
    k = np.swapaxes(k, 1, 2)
    v = np.swapaxes(v, 1, 2)
    scale_mul = np.exp(np.minimum(f64(log_scale_mul), MAX_SCALE_MUL))
    q = l2norm(q) * scale_mul
    k = l2norm(k)
    return q, k, v

@@ -1,0 +1,271 @@
+import math
+from contextlib import ExitStack
+
+import concourse.mybir as mybir
+from concourse.masks import make_identity
+
+F32 = mybir.dt.float32
+BF16 = mybir.dt.bfloat16
+U32 = mybir.dt.uint32
+U8 = mybir.dt.uint8
+FP8X4 = mybir.dt.float8_e4m3fn_x4
+ALU = mybir.AluOpType
+ACT = mybir.ActivationFunctionType
+
+P = 128
+BATCHES, TOKENS, FEATURES, HEADS = 8, 512, 512, 8
+HEAD_DIM = FEATURES // HEADS
+WORDS = FEATURES // 2
+PARTS = 3
+Q, K, V = 0, 1, 2
+MAX_LOG_MUL = math.log(100.0)
+EPS = 1e-12
+
+GROUP_BATCHES = 2
+GROUPS = BATCHES // GROUP_BATCHES
+RUN = GROUP_BATCHES * TOKENS // P
+N_TILES = GROUPS * RUN
+PART_TILES = FEATURES // P
+AHEAD = 4
+LAG = 3
+N_STEPS = N_TILES + (PARTS - 1) * LAG
+
+FLOPS = 2 * BATCHES * TOKENS * FEATURES * PARTS * FEATURES
+
+
+def tile_selfattention_pa_t_kernel(
+    tc, x, w_qkv, q_bias, v_bias, log_scale_mul, out_q, out_k, out_v
+):
+    nc = tc.nc
+    outs = [out_q, out_k, out_v]
+    with ExitStack() as ctx:
+        ctx.enter_context(tc.manual_schedule())
+        keep = ctx.enter_context(tc.tile_pool(name="keep", bufs=1))
+        work = ctx.enter_context(tc.tile_pool(name="work", bufs=3))
+        small = ctx.enter_context(tc.tile_pool(name="small", bufs=4))
+        stage = ctx.enter_context(tc.tile_pool(name="stage", bufs=2))
+        psum = ctx.enter_context(tc.psum_pool(name="psum", bufs=1))
+        banks = {"flipped": 2, "acc0": 2, "acc1": 3, "acc2": 1}
+
+        w_raw = keep.tile([P, PARTS * PART_TILES * FEATURES], BF16, name="w_raw")
+        x_raw = [keep.tile([P, RUN * FEATURES], BF16, name="x_raw%d" % g) for g in range(GROUPS)]
+        rows = keep.tile([P, 2 * FEATURES + 64], BF16, name="rows")
+        nc.vector.memset(rows[:], 0.0)
+
+        def load_w(part):
+            nc.sync.dma_start(
+                out=w_raw[:, part * PART_TILES * FEATURES : (part + 1) * PART_TILES * FEATURES].rearrange(
+                    "p (n f) -> p n f", n=PART_TILES
+                ),
+                in_=w_qkv[part * FEATURES : (part + 1) * FEATURES, :].rearrange("(n p) f -> p n f", p=P),
+            )
+
+        def load_x(g):
+            for j in range(GROUP_BATCHES):
+                nc.sync.dma_start(
+                    out=x_raw[g][j:P:GROUP_BATCHES, :],
+                    in_=x[g * GROUP_BATCHES + j].rearrange("(c t) f -> c (t f)", t=RUN),
+                )
+
+        load_w(Q)
+        load_x(0)
+        nc.sync.dma_start(out=rows[0:1, 0:FEATURES], in_=q_bias.rearrange("(o n) -> o n", o=1))
+        nc.sync.dma_start(out=rows[0:1, FEATURES : 2 * FEATURES], in_=v_bias.rearrange("(o n) -> o n", o=1))
+        nc.sync.dma_start(
+            out=rows[0:1, 2 * FEATURES : 2 * FEATURES + HEADS],
+            in_=log_scale_mul.rearrange("a h b c -> a (h b c)"),
+        )
+        load_w(K)
+        load_w(V)
+        for g in range(1, GROUPS):
+            load_x(g)
+
+        ident = keep.tile([P, P], F32, name="ident")
+        make_identity(nc, ident[:])
+        ones = keep.tile([P, P], BF16, name="ones")
+        nc.vector.memset(ones[:], 1.0)
+        shrink = keep.tile([P, 2 * HEADS], F32, name="shrink")
+        nc.vector.memset(shrink[:, HEADS : 2 * HEADS], 1.0)
+
+        w_words = keep.tile([P, PARTS * FEATURES], U32, name="w_words", align_bytes=64)
+        w_scales = keep.tile([P, PARTS * FEATURES], U8, name="w_scales", align_bytes=64)
+        x_words = keep.tile([P, N_TILES * P], U32, name="x_words", align_bytes=64)
+        x_scales = keep.tile([P, N_TILES * P], U8, name="x_scales", align_bytes=64)
+
+        def flip(raw_words):
+            flipped = psum.tile([P, 4 * P], F32, tag="flipped", bufs=banks["flipped"])
+            for piece in range(4):
+                cols = slice(piece * P, (piece + 1) * P)
+                nc.tensor.transpose(flipped[:, cols], raw_words[:, cols], ident[:])
+            return flipped
+
+        def regroup(flipped):
+            grouped = work.tile([P, 8 * P], BF16, tag="grouped", align_bytes=64)
+            nc.scalar.copy(
+                out=grouped[:].bitcast(F32).rearrange("p (j r u) -> p j r u", j=2, u=2),
+                in_=flipped[:].rearrange("p (j u r) -> p j r u", j=2, u=2),
+            )
+            return grouped
+
+        def quantise(grouped, words, scales, first):
+            cols = slice(first, first + 2 * P)
+            nc.vector.quantize_mx(out=words[:, cols].bitcast(FP8X4), scales=scales[:, cols], in_=grouped[:])
+
+        def w_pair(first):
+            return w_raw[:].bitcast(F32)[:, first * WORDS // P : (first + 2 * P) * WORDS // P]
+
+        def x_pair(first_tile):
+            g, t = divmod(first_tile, RUN)
+            return x_raw[g][:].bitcast(F32)[:, t * WORDS : (t + 2) * WORDS]
+
+        def pack_w(part):
+            firsts = [part * FEATURES + pair * 2 * P for pair in range(PART_TILES // 2)]
+            grouped = [regroup(flip(w_pair(first))) for first in firsts]
+            for first, tile_pair in zip(firsts, grouped):
+                quantise(tile_pair, w_words, w_scales, first)
+
+        pack_w(Q)
+        head = [regroup(flip(x_pair(first_tile))) for first_tile in range(0, AHEAD, 2)]
+        for first_tile, tile_pair in zip(range(0, AHEAD, 2), head):
+            quantise(tile_pair, x_words, x_scales, first_tile * P)
+
+        def spread(first, width):
+            acc = psum.tile([P, FEATURES], F32, tag="acc1", bufs=banks["acc1"])
+            nc.tensor.matmul(acc[:, 0:width], lhsT=ones[:], rhs=rows[:, first : first + width], start=True, stop=True)
+            return acc
+
+        bias_all = {}
+        for part, first in ((Q, 0), (V, FEATURES)):
+            bias_all[part] = keep.tile([P, FEATURES], F32, name="bias_all%d" % part)
+            nc.vector.tensor_copy(out=bias_all[part][:], in_=spread(first, FEATURES)[:])
+        log_mul = keep.tile([P, HEADS], F32, name="log_mul")
+        nc.vector.tensor_scalar_min(out=log_mul[:], in0=spread(2 * FEATURES, 64)[:, 0:HEADS], scalar1=MAX_LOG_MUL)
+        nc.scalar.activation(out=shrink[:, 0:HEADS], in_=log_mul[:], func=ACT.Exp, scale=-2.0)
+
+
+        def tile_of(part, step):
+            index = step - part * LAG
+            return index if 0 <= index < N_TILES else None
+
+        acc = {}
+        staged = {}
+        norm2, shrunk, norm, gain = {}, {}, {}, {}
+        squares = {}
+
+        def by_head(ap):
+            return ap.rearrange("p (h d) -> p h d", h=HEADS)
+
+        def over_head(gain_cols):
+            return gain_cols.unsqueeze(2).to_broadcast([P, HEADS, HEAD_DIM])
+
+        def slot(part, step):
+            g, t = divmod(tile_of(part, step), RUN)
+            return staged[(part, g)][:, :, t, :]
+
+        def project(step):
+            for part in range(PARTS):
+                index = tile_of(part, step)
+                if index is None:
+                    continue
+                bank = psum.tile([P, FEATURES], F32, tag="acc%d" % part, bufs=banks["acc%d" % part])
+                nc.tensor.matmul_mx(
+                    out=bank[:],
+                    lhsT=x_words[:, index * P : (index + 1) * P].bitcast(FP8X4),
+                    lhsT_scale=x_scales[:, index * P : (index + 1) * P],
+                    rhs=w_words[:, part * FEATURES : (part + 1) * FEATURES].bitcast(FP8X4),
+                    rhs_scale=w_scales[:, part * FEATURES : (part + 1) * FEATURES],
+                    start=True,
+                    stop=True,
+                )
+                acc[(part, step)] = bank
+
+        def new_stage(part, step):
+            index = tile_of(part, step)
+            if index is not None and index % RUN == 0:
+                staged[(part, index // RUN)] = stage.tile(
+                    [P, HEADS, RUN, HEAD_DIM], F32, name="staged%d" % part, tag="staged%d" % part
+                )
+
+        def add_bias(part, step):
+            if tile_of(part, step) is None:
+                return
+            new_stage(part, step)
+            nc.vector.tensor_tensor(
+                out=slot(part, step), in0=by_head(acc[(part, step)][:]), in1=by_head(bias_all[part][:]), op=ALU.add
+            )
+
+        def sum_squares(part, step):
+            if tile_of(part, step) is None:
+                return
+            for h in range(HEADS):
+                cols = slice(h * HEAD_DIM, (h + 1) * HEAD_DIM)
+                nc.scalar.activation(
+                    out=squares[step][:, part * FEATURES + h * HEAD_DIM : part * FEATURES + (h + 1) * HEAD_DIM],
+                    in_=slot(Q, step)[:, h, :] if part == Q else acc[(K, step)][:, cols],
+                    func=ACT.Square,
+                    accum_out=norm2[step][:, part * HEADS + h : part * HEADS + h + 1],
+                )
+
+        def live(step):
+            parts = [part for part in (Q, K) if tile_of(part, step) is not None]
+            return slice(parts[0] * HEADS, (parts[-1] + 1) * HEADS) if parts else None
+
+        def store(part, step):
+            index = tile_of(part, step)
+            if index is None or index % RUN != RUN - 1:
+                return
+            for j in range(GROUP_BATCHES):
+                nc.sync.dma_start(
+                    out=outs[part][(index // RUN) * GROUP_BATCHES + j].rearrange("h (c t) d -> c h (t d)", t=RUN),
+                    in_=staged[(part, index // RUN)][j:P:GROUP_BATCHES].rearrange("p h t d -> p h (t d)"),
+                )
+
+        project(0)
+        waiting = None
+        for step in range(N_STEPS):
+            before = step - 1
+            packs = step % 2 == 0 and step + AHEAD < N_TILES
+            if packs:
+                flipped = flip(x_pair(step + AHEAD))
+            project(step + 1)
+
+            if live(step) is not None:
+                squares[step] = work.tile([P, 2 * FEATURES], BF16, name="squares", tag="squares")
+                norm2[step] = small.tile([P, 2 * HEADS], F32, name="norm2", tag="norm2")
+            add_bias(Q, step)
+            new_stage(K, step)
+            sum_squares(K, step)
+            cols = live(before)
+            if cols is not None:
+                shrunk[before] = small.tile([P, 2 * HEADS], F32, name="shrunk", tag="shrunk")
+                nc.vector.scalar_tensor_tensor(
+                    out=shrunk[before][:, cols], in0=norm2[before][:, cols], scalar=EPS * EPS, in1=shrink[:, cols],
+                    op0=ALU.max, op1=ALU.mult,
+                )
+                norm[before] = small.tile([P, 2 * HEADS], F32, name="norm", tag="norm")
+                nc.scalar.activation(out=norm[before][:, cols], in_=shrunk[before][:, cols], func=ACT.Sqrt)
+            add_bias(V, step)
+            store(V, step)
+            sum_squares(Q, step)
+            if cols is not None:
+                gain[before] = small.tile([P, 2 * HEADS], F32, name="gain", tag="gain")
+                nc.vector.reciprocal(out=gain[before][:, cols], in_=norm[before][:, cols])
+            if tile_of(K, before) is not None:
+                nc.vector.tensor_tensor(
+                    out=slot(K, before), in0=by_head(acc[(K, before)][:]),
+                    in1=over_head(gain[before][:, HEADS : 2 * HEADS]), op=ALU.mult,
+                )
+                store(K, before)
+            if tile_of(Q, before) is not None:
+                nc.gpsimd.tensor_tensor(
+                    out=slot(Q, before), in0=slot(Q, before), in1=over_head(gain[before][:, 0:HEADS]), op=ALU.mult
+                )
+                store(Q, before)
+            if waiting is not None:
+                quantise(waiting[0], x_words, x_scales, waiting[1] * P)
+                waiting = None
+            if packs:
+                waiting = (regroup(flipped), step + AHEAD)
+            for part in (K, V):
+                if step == (part - 1) * LAG:
+                    pack_w(part)

@@ -11,6 +11,7 @@ U8 = mybir.dt.uint8
 FP8X4 = mybir.dt.float8_e4m3fn_x4
 ALU = mybir.AluOpType
 ACT = mybir.ActivationFunctionType
+AXIS = mybir.AxisListType
 
 P = 128
 BATCHES, TOKENS, FEATURES, HEADS = 8, 512, 512, 8
@@ -51,6 +52,12 @@ def tile_selfattention_pa_t_kernel(
         x_raw = [keep.tile([P, RUN * FEATURES], BF16, name="x_raw%d" % g) for g in range(GROUPS)]
         rows = keep.tile([P, 2 * FEATURES + 64], BF16, name="rows")
         nc.vector.memset(rows[:], 0.0)
+        nc.scalar.dma_start(out=rows[0:1, 0:FEATURES], in_=q_bias.rearrange("(o n) -> o n", o=1))
+        nc.scalar.dma_start(out=rows[0:1, FEATURES : 2 * FEATURES], in_=v_bias.rearrange("(o n) -> o n", o=1))
+        nc.scalar.dma_start(
+            out=rows[0:1, 2 * FEATURES : 2 * FEATURES + HEADS],
+            in_=log_scale_mul.rearrange("a h b c -> a (h b c)"),
+        )
 
         def load_w(part):
             nc.sync.dma_start(
@@ -69,12 +76,6 @@ def tile_selfattention_pa_t_kernel(
 
         load_w(Q)
         load_x(0)
-        nc.sync.dma_start(out=rows[0:1, 0:FEATURES], in_=q_bias.rearrange("(o n) -> o n", o=1))
-        nc.sync.dma_start(out=rows[0:1, FEATURES : 2 * FEATURES], in_=v_bias.rearrange("(o n) -> o n", o=1))
-        nc.sync.dma_start(
-            out=rows[0:1, 2 * FEATURES : 2 * FEATURES + HEADS],
-            in_=log_scale_mul.rearrange("a h b c -> a (h b c)"),
-        )
         load_w(K)
         load_w(V)
         for g in range(1, GROUPS):
@@ -142,15 +143,14 @@ def tile_selfattention_pa_t_kernel(
         nc.vector.tensor_scalar_min(out=log_mul[:], in0=spread(2 * FEATURES, 64)[:, 0:HEADS], scalar1=MAX_LOG_MUL)
         nc.scalar.activation(out=shrink[:, 0:HEADS], in_=log_mul[:], func=ACT.Exp, scale=-2.0)
 
-
         def tile_of(part, step):
             index = step - part * LAG
             return index if 0 <= index < N_TILES else None
 
         acc = {}
         staged = {}
-        norm2, shrunk, norm, gain = {}, {}, {}, {}
-        squares = {}
+        q_squares = {}
+        norm2, shrunk, gain = {}, {}, {}
 
         def by_head(ap):
             return ap.rearrange("p (h d) -> p h d", h=HEADS)
@@ -194,17 +194,29 @@ def tile_selfattention_pa_t_kernel(
                 out=slot(part, step), in0=by_head(acc[(part, step)][:]), in1=by_head(bias_all[part][:]), op=ALU.add
             )
 
-        def sum_squares(part, step):
-            if tile_of(part, step) is None:
+        def k_norms(step):
+            if tile_of(K, step) is None:
                 return
+            unread = work.tile([P, FEATURES], BF16, tag="unread")
             for h in range(HEADS):
                 cols = slice(h * HEAD_DIM, (h + 1) * HEAD_DIM)
                 nc.scalar.activation(
-                    out=squares[step][:, part * FEATURES + h * HEAD_DIM : part * FEATURES + (h + 1) * HEAD_DIM],
-                    in_=slot(Q, step)[:, h, :] if part == Q else acc[(K, step)][:, cols],
+                    out=unread[:, cols],
+                    in_=acc[(K, step)][:, cols],
                     func=ACT.Square,
-                    accum_out=norm2[step][:, part * HEADS + h : part * HEADS + h + 1],
+                    accum_out=norm2[step][:, HEADS + h : HEADS + h + 1],
                 )
+
+        def square_q(step):
+            if tile_of(Q, step) is None:
+                return
+            q_squares[step] = work.tile([P, HEADS, HEAD_DIM], F32, name="q_squares", tag="q_squares")
+            nc.scalar.activation(out=q_squares[step][:], in_=slot(Q, step), func=ACT.Square)
+
+        def q_norms(step):
+            if tile_of(Q, step) is None:
+                return
+            nc.vector.tensor_reduce(out=norm2[step][:, 0:HEADS], in_=q_squares[step][:], axis=AXIS.X, op=ALU.add)
 
         def live(step):
             parts = [part for part in (Q, K) if tile_of(part, step) is not None]
@@ -230,11 +242,11 @@ def tile_selfattention_pa_t_kernel(
             project(step + 1)
 
             if live(step) is not None:
-                squares[step] = work.tile([P, 2 * FEATURES], BF16, name="squares", tag="squares")
                 norm2[step] = small.tile([P, 2 * HEADS], F32, name="norm2", tag="norm2")
             add_bias(Q, step)
             new_stage(K, step)
-            sum_squares(K, step)
+            k_norms(step)
+            q_norms(before)
             cols = live(before)
             if cols is not None:
                 shrunk[before] = small.tile([P, 2 * HEADS], F32, name="shrunk", tag="shrunk")
@@ -242,14 +254,14 @@ def tile_selfattention_pa_t_kernel(
                     out=shrunk[before][:, cols], in0=norm2[before][:, cols], scalar=EPS * EPS, in1=shrink[:, cols],
                     op0=ALU.max, op1=ALU.mult,
                 )
-                norm[before] = small.tile([P, 2 * HEADS], F32, name="norm", tag="norm")
-                nc.scalar.activation(out=norm[before][:, cols], in_=shrunk[before][:, cols], func=ACT.Sqrt)
+                gain[before] = small.tile([P, 2 * HEADS], F32, name="gain", tag="gain")
+                nc.scalar.activation(out=gain[before][:, cols], in_=shrunk[before][:, cols], func=ACT.Abs_reciprocal_sqrt)
+            square_q(step)
             add_bias(V, step)
             store(V, step)
-            sum_squares(Q, step)
-            if cols is not None:
-                gain[before] = small.tile([P, 2 * HEADS], F32, name="gain", tag="gain")
-                nc.vector.reciprocal(out=gain[before][:, cols], in_=norm[before][:, cols])
+            if waiting is not None:
+                quantise(waiting[0], x_words, x_scales, waiting[1] * P)
+                waiting = None
             if tile_of(K, before) is not None:
                 nc.vector.tensor_tensor(
                     out=slot(K, before), in0=by_head(acc[(K, before)][:]),
@@ -261,9 +273,6 @@ def tile_selfattention_pa_t_kernel(
                     out=slot(Q, before), in0=slot(Q, before), in1=over_head(gain[before][:, 0:HEADS]), op=ALU.mult
                 )
                 store(Q, before)
-            if waiting is not None:
-                quantise(waiting[0], x_words, x_scales, waiting[1] * P)
-                waiting = None
             if packs:
                 waiting = (regroup(flipped), step + AHEAD)
             for part in (K, V):

@@ -28,6 +28,7 @@ RUN = GROUP_BATCHES * TOKENS // P
 N_TILES = GROUPS * RUN
 PART_TILES = FEATURES // P
 AHEAD = 4
+STORE_HEADS = 4
 LAG = 3
 N_STEPS = N_TILES + (PARTS - 1) * LAG
 
@@ -227,10 +228,14 @@ def tile_selfattention_pa_t_kernel(
             if index is None or index % RUN != RUN - 1:
                 return
             for j in range(GROUP_BATCHES):
-                nc.sync.dma_start(
-                    out=outs[part][(index // RUN) * GROUP_BATCHES + j].rearrange("h (c t) d -> c h (t d)", t=RUN),
-                    in_=staged[(part, index // RUN)][j:P:GROUP_BATCHES].rearrange("p h t d -> p h (t d)"),
-                )
+                for first_head in range(0, HEADS, STORE_HEADS):
+                    heads = slice(first_head, first_head + STORE_HEADS)
+                    nc.sync.dma_start(
+                        out=outs[part][(index // RUN) * GROUP_BATCHES + j, heads].rearrange(
+                            "h (c t) d -> c h (t d)", t=RUN
+                        ),
+                        in_=staged[(part, index // RUN)][j:P:GROUP_BATCHES, heads].rearrange("p h t d -> p h (t d)"),
+                    )
 
         project(0)
         waiting = None

@@ -26,11 +26,15 @@ GROUP_BATCHES = 2
 GROUPS = BATCHES // GROUP_BATCHES
 RUN = GROUP_BATCHES * TOKENS // P
 N_TILES = GROUPS * RUN
-PART_TILES = FEATURES // P
+PAIRS = FEATURES // (2 * P)
 AHEAD = 4
-STORE_HEADS = 4
 LAG = 3
 N_STEPS = N_TILES + (PARTS - 1) * LAG
+TAIL_TILES = 2
+
+Q_WIDE_HEADS = 3
+FIRST = HEADS - Q_WIDE_HEADS
+NORM_COLS = FIRST + 2 * HEADS
 
 FLOPS = 2 * BATCHES * TOKENS * FEATURES * PARTS * FEATURES
 
@@ -49,45 +53,55 @@ def tile_selfattention_pa_t_kernel(
         psum = ctx.enter_context(tc.psum_pool(name="psum", bufs=1))
         banks = {"flipped": 2, "acc0": 2, "acc1": 3, "acc2": 1}
 
-        w_raw = keep.tile([P, PARTS * PART_TILES * FEATURES], BF16, name="w_raw")
+        dummy = keep.tile([P, 2], F32, name="dummy")
+        nc.vector.memset(dummy[:], 0.0)
+        nc.scalar.activation(out=dummy[:, 1:2], in_=dummy[:, 0:1], func=ACT.Exp)
+
+        w_raw = keep.tile([P, PARTS * PAIRS * 2 * FEATURES], BF16, name="w_raw")
         x_raw = [keep.tile([P, RUN * FEATURES], BF16, name="x_raw%d" % g) for g in range(GROUPS)]
         rows = keep.tile([P, 2 * FEATURES + 64], BF16, name="rows")
         nc.vector.memset(rows[:], 0.0)
         nc.scalar.dma_start(out=rows[0:1, 0:FEATURES], in_=q_bias.rearrange("(o n) -> o n", o=1))
-        nc.scalar.dma_start(out=rows[0:1, FEATURES : 2 * FEATURES], in_=v_bias.rearrange("(o n) -> o n", o=1))
         nc.scalar.dma_start(
             out=rows[0:1, 2 * FEATURES : 2 * FEATURES + HEADS],
             in_=log_scale_mul.rearrange("a h b c -> a (h b c)"),
         )
+        nc.scalar.dma_start(out=rows[0:1, FEATURES : 2 * FEATURES], in_=v_bias.rearrange("(o n) -> o n", o=1))
 
-        def load_w(part):
+        def load_w(part, pair):
+            first = (part * PAIRS + pair) * 2 * P
             nc.sync.dma_start(
-                out=w_raw[:, part * PART_TILES * FEATURES : (part + 1) * PART_TILES * FEATURES].rearrange(
-                    "p (n f) -> p n f", n=PART_TILES
+                out=w_raw[:, first * FEATURES // P : (first + 2 * P) * FEATURES // P].rearrange(
+                    "p (n f) -> p n f", n=2
                 ),
-                in_=w_qkv[part * FEATURES : (part + 1) * FEATURES, :].rearrange("(n p) f -> p n f", p=P),
+                in_=w_qkv[first : first + 2 * P, :].rearrange("(n p) f -> p n f", p=P),
             )
 
-        def load_x(g):
+        def load_x(g, first_t, n_t):
             for j in range(GROUP_BATCHES):
                 nc.sync.dma_start(
-                    out=x_raw[g][j:P:GROUP_BATCHES, :],
-                    in_=x[g * GROUP_BATCHES + j].rearrange("(c t) f -> c (t f)", t=RUN),
+                    out=x_raw[g][j:P:GROUP_BATCHES, first_t * FEATURES : (first_t + n_t) * FEATURES].rearrange(
+                        "p (t f) -> p t f", f=FEATURES
+                    ),
+                    in_=x[g * GROUP_BATCHES + j].rearrange("(c t) f -> c t f", t=RUN)[:, first_t : first_t + n_t, :],
                 )
 
-        load_w(Q)
-        load_x(0)
-        load_w(K)
-        load_w(V)
+        load_w(Q, 0)
+        load_x(0, 0, 2)
+        load_w(Q, 1)
+        load_x(0, 2, RUN - 2)
+        for part in (K, V):
+            for pair in range(PAIRS):
+                load_w(part, pair)
         for g in range(1, GROUPS):
-            load_x(g)
+            load_x(g, 0, RUN)
 
         ident = keep.tile([P, P], F32, name="ident")
         make_identity(nc, ident[:])
         ones = keep.tile([P, P], BF16, name="ones")
         nc.vector.memset(ones[:], 1.0)
-        shrink = keep.tile([P, 2 * HEADS], F32, name="shrink")
-        nc.vector.memset(shrink[:, HEADS : 2 * HEADS], 1.0)
+        shrink = keep.tile([P, NORM_COLS], F32, name="shrink")
+        nc.vector.memset(shrink[:], 1.0)
 
         w_words = keep.tile([P, PARTS * FEATURES], U32, name="w_words", align_bytes=64)
         w_scales = keep.tile([P, PARTS * FEATURES], U8, name="w_scales", align_bytes=64)
@@ -113,36 +127,45 @@ def tile_selfattention_pa_t_kernel(
             cols = slice(first, first + 2 * P)
             nc.vector.quantize_mx(out=words[:, cols].bitcast(FP8X4), scales=scales[:, cols], in_=grouped[:])
 
-        def w_pair(first):
-            return w_raw[:].bitcast(F32)[:, first * WORDS // P : (first + 2 * P) * WORDS // P]
+        def regrouped_w(part, pair):
+            first = (part * PAIRS + pair) * 2 * P
+            raw_words = w_raw[:].bitcast(F32)[:, first * WORDS // P : (first + 2 * P) * WORDS // P]
+            return regroup(flip(raw_words)), w_words, w_scales, first
 
         def x_pair(first_tile):
             g, t = divmod(first_tile, RUN)
             return x_raw[g][:].bitcast(F32)[:, t * WORDS : (t + 2) * WORDS]
 
-        def pack_w(part):
-            firsts = [part * FEATURES + pair * 2 * P for pair in range(PART_TILES // 2)]
-            grouped = [regroup(flip(w_pair(first))) for first in firsts]
-            for first, tile_pair in zip(firsts, grouped):
-                quantise(tile_pair, w_words, w_scales, first)
+        def regrouped_x(first_tile):
+            return regroup(flip(x_pair(first_tile))), x_words, x_scales, first_tile * P
 
-        pack_w(Q)
-        head = [regroup(flip(x_pair(first_tile))) for first_tile in range(0, AHEAD, 2)]
-        for first_tile, tile_pair in zip(range(0, AHEAD, 2), head):
-            quantise(tile_pair, x_words, x_scales, first_tile * P)
-
-        def spread(first, width):
-            acc = psum.tile([P, FEATURES], F32, tag="acc1", bufs=banks["acc1"])
+        def spread(first, width, tag):
+            acc = psum.tile([P, FEATURES], F32, tag=tag, bufs=banks[tag])
             nc.tensor.matmul(acc[:, 0:width], lhsT=ones[:], rhs=rows[:, first : first + width], start=True, stop=True)
             return acc
 
         bias_all = {}
-        for part, first in ((Q, 0), (V, FEATURES)):
+
+        def spread_bias(part, first):
             bias_all[part] = keep.tile([P, FEATURES], F32, name="bias_all%d" % part)
-            nc.vector.tensor_copy(out=bias_all[part][:], in_=spread(first, FEATURES)[:])
+            nc.vector.tensor_copy(out=bias_all[part][:], in_=spread(first, FEATURES, "acc%d" % part)[:])
+
+        def norm_cols(part):
+            return slice(FIRST + part * HEADS, FIRST + (part + 1) * HEADS)
+
+        w_first = regrouped_w(Q, 0)
+        x_first = regrouped_x(0)
+        quantise(*w_first)
+        w_second = regrouped_w(Q, 1)
+        quantise(*x_first)
+        waiting = regrouped_x(2)
+        quantise(*w_second)
+        spread_bias(Q, 0)
         log_mul = keep.tile([P, HEADS], F32, name="log_mul")
-        nc.vector.tensor_scalar_min(out=log_mul[:], in0=spread(2 * FEATURES, 64)[:, 0:HEADS], scalar1=MAX_LOG_MUL)
-        nc.scalar.activation(out=shrink[:, 0:HEADS], in_=log_mul[:], func=ACT.Exp, scale=-2.0)
+        nc.vector.tensor_scalar_min(
+            out=log_mul[:], in0=spread(2 * FEATURES, 64, "acc0")[:, 0:HEADS], scalar1=MAX_LOG_MUL
+        )
+        nc.scalar.activation(out=shrink[:, norm_cols(Q)], in_=log_mul[:], func=ACT.Exp, scale=-2.0)
 
         def tile_of(part, step):
             index = step - part * LAG
@@ -150,6 +173,7 @@ def tile_selfattention_pa_t_kernel(
 
         acc = {}
         staged = {}
+        unread = {}
         q_squares = {}
         norm2, shrunk, gain = {}, {}, {}
 
@@ -195,50 +219,35 @@ def tile_selfattention_pa_t_kernel(
                 out=slot(part, step), in0=by_head(acc[(part, step)][:]), in1=by_head(bias_all[part][:]), op=ALU.add
             )
 
-        def k_norms(step):
-            if tile_of(K, step) is None:
-                return
-            unread = work.tile([P, FEATURES], BF16, tag="unread")
-            for h in range(HEADS):
-                cols = slice(h * HEAD_DIM, (h + 1) * HEAD_DIM)
+        def one_head_norms(part, step, heads, values):
+            for h in heads:
                 nc.scalar.activation(
-                    out=unread[:, cols],
-                    in_=acc[(K, step)][:, cols],
+                    out=unread[step][:, part * HEADS + h, :],
+                    in_=values[:, h, :],
                     func=ACT.Square,
-                    accum_out=norm2[step][:, HEADS + h : HEADS + h + 1],
+                    accum_out=norm2[step][:, FIRST + part * HEADS + h : FIRST + part * HEADS + h + 1],
                 )
-
-        def square_q(step):
-            if tile_of(Q, step) is None:
-                return
-            q_squares[step] = work.tile([P, HEADS, HEAD_DIM], F32, name="q_squares", tag="q_squares")
-            nc.scalar.activation(out=q_squares[step][:], in_=slot(Q, step), func=ACT.Square)
-
-        def q_norms(step):
-            if tile_of(Q, step) is None:
-                return
-            nc.vector.tensor_reduce(out=norm2[step][:, 0:HEADS], in_=q_squares[step][:], axis=AXIS.X, op=ALU.add)
 
         def live(step):
             parts = [part for part in (Q, K) if tile_of(part, step) is not None]
-            return slice(parts[0] * HEADS, (parts[-1] + 1) * HEADS) if parts else None
+            return slice(FIRST + parts[0] * HEADS, FIRST + (parts[-1] + 1) * HEADS) if parts else None
 
-        def store(part, step):
+        def store_finished(part, step):
             index = tile_of(part, step)
-            if index is None or index % RUN != RUN - 1:
+            if index is None:
                 return
+            g, t = divmod(index, RUN)
+            n_t = RUN if g < GROUPS - 1 else TAIL_TILES
+            if (t + 1) % n_t != 0:
+                return
+            tokens = slice(t + 1 - n_t, t + 1)
             for j in range(GROUP_BATCHES):
-                for first_head in range(0, HEADS, STORE_HEADS):
-                    heads = slice(first_head, first_head + STORE_HEADS)
-                    nc.sync.dma_start(
-                        out=outs[part][(index // RUN) * GROUP_BATCHES + j, heads].rearrange(
-                            "h (c t) d -> c h (t d)", t=RUN
-                        ),
-                        in_=staged[(part, index // RUN)][j:P:GROUP_BATCHES, heads].rearrange("p h t d -> p h (t d)"),
-                    )
+                nc.sync.dma_start(
+                    out=outs[part][g * GROUP_BATCHES + j].rearrange("h (c t) d -> c h t d", t=RUN)[:, :, tokens, :],
+                    in_=staged[(part, g)][j:P:GROUP_BATCHES, :, tokens, :],
+                )
 
         project(0)
-        waiting = None
         for step in range(N_STEPS):
             before = step - 1
             packs = step % 2 == 0 and step + AHEAD < N_TILES
@@ -247,39 +256,52 @@ def tile_selfattention_pa_t_kernel(
             project(step + 1)
 
             if live(step) is not None:
-                norm2[step] = small.tile([P, 2 * HEADS], F32, name="norm2", tag="norm2")
+                norm2[step] = small.tile([P, NORM_COLS], F32, name="norm2", tag="norm2")
+                unread[step] = work.tile([P, 2 * HEADS, HEAD_DIM], BF16, name="unread", tag="unread")
             add_bias(Q, step)
             new_stage(K, step)
-            k_norms(step)
-            q_norms(before)
+            if tile_of(K, step) is not None:
+                one_head_norms(K, step, range(HEADS), by_head(acc[(K, step)][:]))
+            if tile_of(Q, before) is not None:
+                nc.vector.tensor_reduce(
+                    out=norm2[before][:, FIRST:HEADS], in_=q_squares[before][:], axis=AXIS.X, op=ALU.add
+                )
             cols = live(before)
             if cols is not None:
-                shrunk[before] = small.tile([P, 2 * HEADS], F32, name="shrunk", tag="shrunk")
+                shrunk[before] = small.tile([P, NORM_COLS], F32, name="shrunk", tag="shrunk")
                 nc.vector.scalar_tensor_tensor(
                     out=shrunk[before][:, cols], in0=norm2[before][:, cols], scalar=EPS * EPS, in1=shrink[:, cols],
                     op0=ALU.max, op1=ALU.mult,
                 )
-                gain[before] = small.tile([P, 2 * HEADS], F32, name="gain", tag="gain")
+                gain[before] = small.tile([P, NORM_COLS], F32, name="gain", tag="gain")
                 nc.scalar.activation(out=gain[before][:, cols], in_=shrunk[before][:, cols], func=ACT.Abs_reciprocal_sqrt)
-            square_q(step)
+            if tile_of(Q, step) is not None:
+                q_squares[step] = work.tile([P, Q_WIDE_HEADS, HEAD_DIM], F32, name="q_squares", tag="q_squares")
+                nc.scalar.activation(out=q_squares[step][:], in_=slot(Q, step)[:, 0:Q_WIDE_HEADS, :], func=ACT.Square)
+                one_head_norms(Q, step, range(Q_WIDE_HEADS, HEADS), slot(Q, step))
             add_bias(V, step)
-            store(V, step)
+            store_finished(V, step)
             if waiting is not None:
-                quantise(waiting[0], x_words, x_scales, waiting[1] * P)
+                quantise(*waiting)
                 waiting = None
             if tile_of(K, before) is not None:
                 nc.vector.tensor_tensor(
                     out=slot(K, before), in0=by_head(acc[(K, before)][:]),
-                    in1=over_head(gain[before][:, HEADS : 2 * HEADS]), op=ALU.mult,
+                    in1=over_head(gain[before][:, norm_cols(K)]), op=ALU.mult,
                 )
-                store(K, before)
+                store_finished(K, before)
             if tile_of(Q, before) is not None:
                 nc.gpsimd.tensor_tensor(
-                    out=slot(Q, before), in0=slot(Q, before), in1=over_head(gain[before][:, 0:HEADS]), op=ALU.mult
+                    out=slot(Q, before), in0=slot(Q, before), in1=over_head(gain[before][:, norm_cols(Q)]), op=ALU.mult
                 )
-                store(Q, before)
+                store_finished(Q, before)
             if packs:
-                waiting = (regroup(flipped), step + AHEAD)
+                waiting = (regroup(flipped), x_words, x_scales, (step + AHEAD) * P)
             for part in (K, V):
                 if step == (part - 1) * LAG:
-                    pack_w(part)
+                    w_first = regrouped_w(part, 0)
+                    w_second = regrouped_w(part, 1)
+                    quantise(*w_first)
+                    quantise(*w_second)
+                    if part == V:
+                        spread_bias(V, FEATURES)

@@ -291,7 +291,7 @@ def tile_selfattention_pa_t_kernel(
                 )
                 store_finished(K, before)
             if tile_of(Q, before) is not None:
-                nc.gpsimd.tensor_tensor(
+                nc.vector.tensor_tensor(
                     out=slot(Q, before), in0=slot(Q, before), in1=over_head(gain[before][:, norm_cols(Q)]), op=ALU.mult
                 )
                 store_finished(Q, before)

@@ -51,7 +51,7 @@ def tile_selfattention_pa_t_kernel(
         small = ctx.enter_context(tc.tile_pool(name="small", bufs=4))
         stage = ctx.enter_context(tc.tile_pool(name="stage", bufs=2))
         psum = ctx.enter_context(tc.psum_pool(name="psum", bufs=1))
-        banks = {"flipped": 2, "acc0": 2, "acc1": 3, "acc2": 1}
+        banks = {"flipped": 2, "acc0": 1, "acc1": 4, "acc2": 1}
 
         dummy = keep.tile([P, 2], F32, name="dummy")
         nc.vector.memset(dummy[:], 0.0)
@@ -250,6 +250,7 @@ def tile_selfattention_pa_t_kernel(
         project(0)
         for step in range(N_STEPS):
             before = step - 1
+            earlier = step - 2
             packs = step % 2 == 0 and step + AHEAD < N_TILES
             if packs:
                 flipped = flip(x_pair(step + AHEAD))
@@ -273,25 +274,26 @@ def tile_selfattention_pa_t_kernel(
                     out=shrunk[before][:, cols], in0=norm2[before][:, cols], scalar=EPS * EPS, in1=shrink[:, cols],
                     op0=ALU.max, op1=ALU.mult,
                 )
-                gain[before] = small.tile([P, NORM_COLS], F32, name="gain", tag="gain")
-                nc.scalar.activation(out=gain[before][:, cols], in_=shrunk[before][:, cols], func=ACT.Abs_reciprocal_sqrt)
             if tile_of(Q, step) is not None:
                 q_squares[step] = work.tile([P, Q_WIDE_HEADS, HEAD_DIM], F32, name="q_squares", tag="q_squares")
                 nc.scalar.activation(out=q_squares[step][:], in_=slot(Q, step)[:, 0:Q_WIDE_HEADS, :], func=ACT.Square)
                 one_head_norms(Q, step, range(Q_WIDE_HEADS, HEADS), slot(Q, step))
+            if cols is not None:
+                gain[before] = small.tile([P, NORM_COLS], F32, name="gain", tag="gain")
+                nc.scalar.activation(out=gain[before][:, cols], in_=shrunk[before][:, cols], func=ACT.Abs_reciprocal_sqrt)
             add_bias(V, step)
             store_finished(V, step)
             if waiting is not None:
                 quantise(*waiting)
                 waiting = None
-            if tile_of(K, before) is not None:
+            if tile_of(K, earlier) is not None:
                 nc.vector.tensor_tensor(
-                    out=slot(K, before), in0=by_head(acc[(K, before)][:]),
-                    in1=over_head(gain[before][:, norm_cols(K)]), op=ALU.mult,
+                    out=slot(K, earlier), in0=by_head(acc[(K, earlier)][:]),
+                    in1=over_head(gain[earlier][:, norm_cols(K)]), op=ALU.mult,
                 )
-                store_finished(K, before)
+                store_finished(K, earlier)
             if tile_of(Q, before) is not None:
-                nc.vector.tensor_tensor(
+                nc.gpsimd.tensor_tensor(
                     out=slot(Q, before), in0=slot(Q, before), in1=over_head(gain[before][:, norm_cols(Q)]), op=ALU.mult
                 )
                 store_finished(Q, before)

import math
from contextlib import ExitStack

import concourse.mybir as mybir
from concourse.masks import make_identity

F32 = mybir.dt.float32
BF16 = mybir.dt.bfloat16
U32 = mybir.dt.uint32
U8 = mybir.dt.uint8
FP8X4 = mybir.dt.float8_e4m3fn_x4
ALU = mybir.AluOpType
ACT = mybir.ActivationFunctionType
AXIS = mybir.AxisListType

P = 128
BATCHES, TOKENS, FEATURES, HEADS = 8, 512, 512, 8
HEAD_DIM = FEATURES // HEADS
WORDS = FEATURES // 2
PARTS = 3
Q, K, V = 0, 1, 2
MAX_LOG_MUL = math.log(100.0)
EPS = 1e-12

GROUP_BATCHES = 2
GROUPS = BATCHES // GROUP_BATCHES
RUN = GROUP_BATCHES * TOKENS // P
N_TILES = GROUPS * RUN
PAIRS = FEATURES // (2 * P)
AHEAD = 4
LAG = 3
N_STEPS = N_TILES + (PARTS - 1) * LAG
TAIL_TILES = 2

Q_WIDE_HEADS = 3
FIRST = HEADS - Q_WIDE_HEADS
NORM_COLS = FIRST + 2 * HEADS

FLOPS = 2 * BATCHES * TOKENS * FEATURES * PARTS * FEATURES


def tile_selfattention_pa_t_kernel(
    tc, x, w_qkv, q_bias, v_bias, log_scale_mul, out_q, out_k, out_v
):
    nc = tc.nc
    outs = [out_q, out_k, out_v]
    with ExitStack() as ctx:
        ctx.enter_context(tc.manual_schedule())
        keep = ctx.enter_context(tc.tile_pool(name="keep", bufs=1))
        work = ctx.enter_context(tc.tile_pool(name="work", bufs=3))
        small = ctx.enter_context(tc.tile_pool(name="small", bufs=4))
        stage = ctx.enter_context(tc.tile_pool(name="stage", bufs=2))
        psum = ctx.enter_context(tc.psum_pool(name="psum", bufs=1))
        banks = {"flipped": 2, "acc0": 1, "acc1": 4, "acc2": 1}

        dummy = keep.tile([P, 2], F32, name="dummy")
        nc.vector.memset(dummy[:], 0.0)
        nc.scalar.activation(out=dummy[:, 1:2], in_=dummy[:, 0:1], func=ACT.Exp)

        w_raw = keep.tile([P, PARTS * PAIRS * 2 * FEATURES], BF16, name="w_raw")
        x_raw = [keep.tile([P, RUN * FEATURES], BF16, name="x_raw%d" % g) for g in range(GROUPS)]
        rows = keep.tile([P, 2 * FEATURES + 64], BF16, name="rows")
        nc.vector.memset(rows[:], 0.0)
        nc.scalar.dma_start(out=rows[0:1, 0:FEATURES], in_=q_bias.rearrange("(o n) -> o n", o=1))
        nc.scalar.dma_start(
            out=rows[0:1, 2 * FEATURES : 2 * FEATURES + HEADS],
            in_=log_scale_mul.rearrange("a h b c -> a (h b c)"),
        )
        nc.scalar.dma_start(out=rows[0:1, FEATURES : 2 * FEATURES], in_=v_bias.rearrange("(o n) -> o n", o=1))

        def load_w(part, pair):
            first = (part * PAIRS + pair) * 2 * P
            nc.sync.dma_start(
                out=w_raw[:, first * FEATURES // P : (first + 2 * P) * FEATURES // P].rearrange(
                    "p (n f) -> p n f", n=2
                ),
                in_=w_qkv[first : first + 2 * P, :].rearrange("(n p) f -> p n f", p=P),
            )

        def load_x(g, first_t, n_t):
            for j in range(GROUP_BATCHES):
                nc.sync.dma_start(
                    out=x_raw[g][j:P:GROUP_BATCHES, first_t * FEATURES : (first_t + n_t) * FEATURES].rearrange(
                        "p (t f) -> p t f", f=FEATURES
                    ),
                    in_=x[g * GROUP_BATCHES + j].rearrange("(c t) f -> c t f", t=RUN)[:, first_t : first_t + n_t, :],
                )

        load_w(Q, 0)
        load_x(0, 0, 2)
        load_w(Q, 1)
        load_x(0, 2, RUN - 2)
        for part in (K, V):
            for pair in range(PAIRS):
                load_w(part, pair)
        for g in range(1, GROUPS):
            load_x(g, 0, RUN)

        ident = keep.tile([P, P], F32, name="ident")
        make_identity(nc, ident[:])
        ones = keep.tile([P, P], BF16, name="ones")
        nc.vector.memset(ones[:], 1.0)
        shrink = keep.tile([P, NORM_COLS], F32, name="shrink")
        nc.vector.memset(shrink[:], 1.0)

        w_words = keep.tile([P, PARTS * FEATURES], U32, name="w_words", align_bytes=64)
        w_scales = keep.tile([P, PARTS * FEATURES], U8, name="w_scales", align_bytes=64)
        x_words = keep.tile([P, N_TILES * P], U32, name="x_words", align_bytes=64)
        x_scales = keep.tile([P, N_TILES * P], U8, name="x_scales", align_bytes=64)

        def flip(raw_words):
            flipped = psum.tile([P, 4 * P], F32, tag="flipped", bufs=banks["flipped"])
            for piece in range(4):
                cols = slice(piece * P, (piece + 1) * P)
                nc.tensor.transpose(flipped[:, cols], raw_words[:, cols], ident[:])
            return flipped

        def regroup(flipped):
            grouped = work.tile([P, 8 * P], BF16, tag="grouped", align_bytes=64)
            nc.scalar.copy(
                out=grouped[:].bitcast(F32).rearrange("p (j r u) -> p j r u", j=2, u=2),
                in_=flipped[:].rearrange("p (j u r) -> p j r u", j=2, u=2),
            )
            return grouped

        def quantise(grouped, words, scales, first):
            cols = slice(first, first + 2 * P)
            nc.vector.quantize_mx(out=words[:, cols].bitcast(FP8X4), scales=scales[:, cols], in_=grouped[:])

        def regrouped_w(part, pair):
            first = (part * PAIRS + pair) * 2 * P
            raw_words = w_raw[:].bitcast(F32)[:, first * WORDS // P : (first + 2 * P) * WORDS // P]
            return regroup(flip(raw_words)), w_words, w_scales, first

        def x_pair(first_tile):
            g, t = divmod(first_tile, RUN)
            return x_raw[g][:].bitcast(F32)[:, t * WORDS : (t + 2) * WORDS]

        def regrouped_x(first_tile):
            return regroup(flip(x_pair(first_tile))), x_words, x_scales, first_tile * P

        def spread(first, width, tag):
            acc = psum.tile([P, FEATURES], F32, tag=tag, bufs=banks[tag])
            nc.tensor.matmul(acc[:, 0:width], lhsT=ones[:], rhs=rows[:, first : first + width], start=True, stop=True)
            return acc

        bias_all = {}

        def spread_bias(part, first):
            bias_all[part] = keep.tile([P, FEATURES], F32, name="bias_all%d" % part)
            nc.vector.tensor_copy(out=bias_all[part][:], in_=spread(first, FEATURES, "acc%d" % part)[:])

        def norm_cols(part):
            return slice(FIRST + part * HEADS, FIRST + (part + 1) * HEADS)

        w_first = regrouped_w(Q, 0)
        x_first = regrouped_x(0)
        quantise(*w_first)
        w_second = regrouped_w(Q, 1)
        quantise(*x_first)
        waiting = regrouped_x(2)
        quantise(*w_second)
        spread_bias(Q, 0)
        log_mul = keep.tile([P, HEADS], F32, name="log_mul")
        nc.vector.tensor_scalar_min(
            out=log_mul[:], in0=spread(2 * FEATURES, 64, "acc0")[:, 0:HEADS], scalar1=MAX_LOG_MUL
        )
        nc.scalar.activation(out=shrink[:, norm_cols(Q)], in_=log_mul[:], func=ACT.Exp, scale=-2.0)

        def tile_of(part, step):
            index = step - part * LAG
            return index if 0 <= index < N_TILES else None

        acc = {}
        staged = {}
        unread = {}
        q_squares = {}
        norm2, shrunk, gain = {}, {}, {}

        def by_head(ap):
            return ap.rearrange("p (h d) -> p h d", h=HEADS)

        def over_head(gain_cols):
            return gain_cols.unsqueeze(2).to_broadcast([P, HEADS, HEAD_DIM])

        def slot(part, step):
            g, t = divmod(tile_of(part, step), RUN)
            return staged[(part, g)][:, :, t, :]

        def project(step):
            for part in range(PARTS):
                index = tile_of(part, step)
                if index is None:
                    continue
                bank = psum.tile([P, FEATURES], F32, tag="acc%d" % part, bufs=banks["acc%d" % part])
                nc.tensor.matmul_mx(
                    out=bank[:],
                    lhsT=x_words[:, index * P : (index + 1) * P].bitcast(FP8X4),
                    lhsT_scale=x_scales[:, index * P : (index + 1) * P],
                    rhs=w_words[:, part * FEATURES : (part + 1) * FEATURES].bitcast(FP8X4),
                    rhs_scale=w_scales[:, part * FEATURES : (part + 1) * FEATURES],
                    start=True,
                    stop=True,
                )
                acc[(part, step)] = bank

        def new_stage(part, step):
            index = tile_of(part, step)
            if index is not None and index % RUN == 0:
                staged[(part, index // RUN)] = stage.tile(
                    [P, HEADS, RUN, HEAD_DIM], F32, name="staged%d" % part, tag="staged%d" % part
                )

        def add_bias(part, step):
            if tile_of(part, step) is None:
                return
            new_stage(part, step)
            nc.vector.tensor_tensor(
                out=slot(part, step), in0=by_head(acc[(part, step)][:]), in1=by_head(bias_all[part][:]), op=ALU.add
            )

        def one_head_norms(part, step, heads, values):
            for h in heads:
                nc.scalar.activation(
                    out=unread[step][:, part * HEADS + h, :],
                    in_=values[:, h, :],
                    func=ACT.Square,
                    accum_out=norm2[step][:, FIRST + part * HEADS + h : FIRST + part * HEADS + h + 1],
                )

        def live(step):
            parts = [part for part in (Q, K) if tile_of(part, step) is not None]
            return slice(FIRST + parts[0] * HEADS, FIRST + (parts[-1] + 1) * HEADS) if parts else None

        def store_finished(part, step):
            index = tile_of(part, step)
            if index is None:
                return
            g, t = divmod(index, RUN)
            n_t = RUN if g < GROUPS - 1 else TAIL_TILES
            if (t + 1) % n_t != 0:
                return
            tokens = slice(t + 1 - n_t, t + 1)
            for j in range(GROUP_BATCHES):
                nc.sync.dma_start(
                    out=outs[part][g * GROUP_BATCHES + j].rearrange("h (c t) d -> c h t d", t=RUN)[:, :, tokens, :],
                    in_=staged[(part, g)][j:P:GROUP_BATCHES, :, tokens, :],
                )

        project(0)
        for step in range(N_STEPS):
            before = step - 1
            earlier = step - 2
            packs = step % 2 == 0 and step + AHEAD < N_TILES
            if packs:
                flipped = flip(x_pair(step + AHEAD))
            project(step + 1)

            if live(step) is not None:
                norm2[step] = small.tile([P, NORM_COLS], F32, name="norm2", tag="norm2")
                unread[step] = work.tile([P, 2 * HEADS, HEAD_DIM], BF16, name="unread", tag="unread")
            add_bias(Q, step)
            new_stage(K, step)
            if tile_of(K, step) is not None:
                one_head_norms(K, step, range(HEADS), by_head(acc[(K, step)][:]))
            if tile_of(Q, before) is not None:
                nc.vector.tensor_reduce(
                    out=norm2[before][:, FIRST:HEADS], in_=q_squares[before][:], axis=AXIS.X, op=ALU.add
                )
            cols = live(before)
            if cols is not None:
                shrunk[before] = small.tile([P, NORM_COLS], F32, name="shrunk", tag="shrunk")
                nc.vector.scalar_tensor_tensor(
                    out=shrunk[before][:, cols], in0=norm2[before][:, cols], scalar=EPS * EPS, in1=shrink[:, cols],
                    op0=ALU.max, op1=ALU.mult,
                )
            if tile_of(Q, step) is not None:
                q_squares[step] = work.tile([P, Q_WIDE_HEADS, HEAD_DIM], F32, name="q_squares", tag="q_squares")
                nc.scalar.activation(out=q_squares[step][:], in_=slot(Q, step)[:, 0:Q_WIDE_HEADS, :], func=ACT.Square)
                one_head_norms(Q, step, range(Q_WIDE_HEADS, HEADS), slot(Q, step))
            if cols is not None:
                gain[before] = small.tile([P, NORM_COLS], F32, name="gain", tag="gain")
                nc.scalar.activation(out=gain[before][:, cols], in_=shrunk[before][:, cols], func=ACT.Abs_reciprocal_sqrt)
            add_bias(V, step)
            store_finished(V, step)
            if waiting is not None:
                quantise(*waiting)
                waiting = None
            if tile_of(K, earlier) is not None:
                nc.vector.tensor_tensor(
                    out=slot(K, earlier), in0=by_head(acc[(K, earlier)][:]),
                    in1=over_head(gain[earlier][:, norm_cols(K)]), op=ALU.mult,
                )
                store_finished(K, earlier)
            if tile_of(Q, before) is not None:
                nc.gpsimd.tensor_tensor(
                    out=slot(Q, before), in0=slot(Q, before), in1=over_head(gain[before][:, norm_cols(Q)]), op=ALU.mult
                )
                store_finished(Q, before)
            if packs:
                waiting = (regroup(flipped), x_words, x_scales, (step + AHEAD) * P)
            for part in (K, V):
                if step == (part - 1) * LAG:
                    w_first = regrouped_w(part, 0)
                    w_second = regrouped_w(part, 1)
                    quantise(*w_first)
                    quantise(*w_second)
                    if part == V:
                        spread_bias(V, FEATURES)
